import numpy as np
import ml_dtypes


def mxq(x, axis, fmt="e4m3"):
    dtype, down = {"e4m3": (ml_dtypes.float8_e4m3fn, 7), "e5m2": (ml_dtypes.float8_e5m2, 14)}[fmt]
    v = np.moveaxis(np.asarray(x, np.float32).astype(ml_dtypes.bfloat16).astype(np.float64), axis, -1)
    blocks = v.reshape(v.shape[:-1] + (-1, 32))
    amax = np.abs(blocks).max(-1, keepdims=True)
    byte = np.maximum(np.where(amax > 0, np.frexp(amax)[1] - 1 + 127, 0) - down, 1)
    scale = np.exp2(byte - 127.0)
    codes = (blocks / scale).astype(np.float32).astype(dtype).astype(np.float64)
    return np.moveaxis((codes * scale).reshape(v.shape), -1, axis)


WIDE = False


def mx_kscale(k):
    if not WIDE:
        return np.ones(k)
    levels = np.array([10, -10, 5, -5, 0])
    if k % 512:
        return np.exp2(np.random.permutation(np.resize(levels, k // 32))).repeat(32)
    a = np.empty((k // 512, 16))
    for p in range(k // 512):
        a[p, :8] = np.random.permutation(np.resize(levels, 8))
        for g in range(8):
            far = levels[np.abs(levels - a[p, g]) >= 10]
            a[p, g + 8] = far[np.random.randint(len(far))]
    return np.exp2(a.ravel()).repeat(32)


BF16 = ml_dtypes.bfloat16


def bf(x):
    return np.asarray(x, np.float32).astype(BF16)


def f64(x):
    return np.asarray(x).astype(np.float64)


E2M1 = np.array([0.0, 0.5, 1.0, 1.5, 2.0, 3.0, 4.0, 6.0, -0.0, -0.5, -1.0, -1.5, -2.0, -3.0, -4.0, -6.0])


def pack_weight(w, fmt):
    k, n = w.shape
    w = f64(bf(w)).reshape(k // 32, 32, n)
    amax = np.abs(w).max(1)
    if fmt == "e4m3":
        byte = np.frexp(amax)[1] - 1 + 127 - 7
    else:
        mant, ex = np.frexp(amax / 6.0)
        byte = np.where(mant > 0.5, ex, ex - 1) + 127
    byte = np.clip(np.where(amax > 0, byte, 1), 1, 254)
    scaled = (w * np.exp2(127.0 - byte)[:, None, :]).reshape(k, n).astype(np.float32)
    by_word = np.ascontiguousarray(scaled.reshape(k // 512, 128, 4, n).transpose(0, 1, 3, 2))
    if fmt == "e4m3":
        words = by_word.astype(ml_dtypes.float8_e4m3fn).view(np.uint8)
    else:
        c = by_word.astype(ml_dtypes.float4_e2m1fn).view(np.uint8) & 0xF
        words = c[..., 0::2] | (c[..., 1::2] << 4)
    return np.ascontiguousarray(words), np.ascontiguousarray(byte.astype(np.uint8).reshape(k // 512, 16, n))


def unpack_weight(words, scales, fmt):
    g, p, n, _ = words.shape
    if fmt == "e4m3":
        vals = np.ascontiguousarray(words).view(ml_dtypes.float8_e4m3fn).astype(np.float64)
    else:
        nib = np.empty((g, p, n, 4), np.uint8)
        nib[..., 0::2] = words & 0xF
        nib[..., 1::2] = words >> 4
        vals = E2M1[nib]
    vals = vals * np.repeat(np.exp2(scales.astype(np.float64) - 127.0), 8, axis=1)[..., None]
    return vals.transpose(0, 1, 3, 2).reshape(g * 512, n)


BS, N, D, B, D_PM = 2, 4096, 512, 8, 512


def setup_inputs():
    k, t = mx_kscale(D_PM), mx_kscale(D_PM)
    w = np.eye(D_PM) / B + 1.6 / np.sqrt(B * D_PM) * np.random.standard_normal((BS, B, D_PM, D_PM))
    pre = bf(np.random.standard_normal((BS, N, D_PM)) * k)
    W_pm = bf(w * t[:, None] / k)
    proj = np.random.standard_normal((D, D_PM)) / np.sqrt(D_PM) / t
    words, scales = pack_weight(proj.T, "e4m3")
    proj_out_b = bf(np.random.standard_normal(D) * 0.3)
    return {"pre": pre,
            "W_pm": W_pm,
            "proj_out_w_words": words,
            "proj_out_w_scales": scales,
            "proj_out_b": proj_out_b}


def reference(pre, W_pm, proj_out_w_words, proj_out_w_scales, proj_out_b):
    W_sum = np.sum(f64(W_pm), axis=1)
    post = mxq(f64(pre), 2, "e4m3") @ mxq(W_sum, 2, "e4m3").transpose(0, 2, 1)
    return (mxq(post, 2, "e4m3") @ unpack_weight(proj_out_w_words, proj_out_w_scales, "e4m3")) + f64(proj_out_b)

@@ -1,0 +1,294 @@
+from contextlib import ExitStack
+
+import concourse.mybir as mybir
+from concourse.masks import make_identity
+
+F32 = mybir.dt.float32
+BF16 = mybir.dt.bfloat16
+I32 = mybir.dt.int32
+U32 = mybir.dt.uint32
+U8 = mybir.dt.uint8
+FP8X4 = mybir.dt.float8_e4m3fn_x4
+ADD = mybir.AluOpType.add
+
+P = 128
+PACK = 4
+SAMPLES = 2
+TOKENS = 4096
+WIDTH = 512
+BANKS = 8
+VECTOR_BANKS = 2
+N_CHUNKS = SAMPLES * TOKENS // (PACK * P)
+N_TILES = N_CHUNKS * PACK
+PAIR = 2
+
+TRANSPOSE_AHEAD = 5
+REGROUP_PRE_AHEAD = 4
+QUANTISE_PRE_AHEAD = 3
+TRANSPOSE_BEFORE_TILE = 3
+FIRST_MATMUL_AHEAD = 9
+REGROUP_POST_AHEAD = 8
+QUANTISE_POST_AHEAD = 5
+SECOND_MATMUL_AHEAD = 3
+
+FLOPS = 2 * 2 * SAMPLES * TOKENS * WIDTH * WIDTH
+
+
+def tile_proceduralmemory_pc_t_kernel(
+    tc, pre, W_pm, proj_out_w_words, proj_out_w_scales, proj_out_b, out
+):
+    nc = tc.nc
+    pre_view = pre.rearrange("b (p s) i -> b p s i", p=P)
+    out_view = out.rearrange("b (p s) n -> b p s n", p=P)
+    mem_view = W_pm.rearrange("b k (p j) i -> b k p j i", j=PACK)
+
+    with ExitStack() as ctx:
+        ctx.enter_context(tc.manual_schedule())
+        const = ctx.enter_context(tc.tile_pool(name="const", bufs=1))
+        mem_pool = ctx.enter_context(tc.tile_pool(name="mem", bufs=BANKS))
+        pre_pool = ctx.enter_context(tc.tile_pool(name="pre", bufs=N_CHUNKS))
+        sum_pool = ctx.enter_context(tc.tile_pool(name="sum", bufs=2))
+        quarter_pool = ctx.enter_context(tc.tile_pool(name="quarter", bufs=PACK))
+        chunk_pool = ctx.enter_context(tc.tile_pool(name="chunk", bufs=4))
+        pair_pool = ctx.enter_context(tc.tile_pool(name="pair", bufs=4))
+        store_pool = ctx.enter_context(tc.tile_pool(name="store", bufs=24))
+        tp_psum = ctx.enter_context(tc.psum_pool(name="tp", bufs=2))
+
+        ident_f32 = const.tile([P, P], F32)
+        make_identity(nc, ident_f32[:])
+        ident_bf = const.tile([P, P], BF16)
+        make_identity(nc, ident_bf[:])
+        ones = const.tile([P, P], BF16)
+        nc.vector.memset(ones[:], 1.0)
+        bias_rows = const.tile([P, WIDTH], BF16)
+        nc.vector.memset(bias_rows[:], 0.0)
+        w_scales = const.tile([P, WIDTH], U8, align_bytes=64)
+        nc.vector.memset(w_scales[:].bitcast(I32), 0)
+        w_codes = const.tile([P, WIDTH], U32, align_bytes=64)
+        bias_all = const.tile([P, WIDTH], F32)
+        mem_codes = [
+            const.tile([P, WIDTH], U32, align_bytes=64, name="mem_codes%d" % b) for b in range(SAMPLES)
+        ]
+        mem_scales = [
+            const.tile([P, WIDTH], U8, align_bytes=64, name="mem_scales%d" % b) for b in range(SAMPLES)
+        ]
+
+        def load_memory(b):
+            banks = []
+            for k in range(BANKS):
+                bank_sb = mem_pool.tile([P, PACK, WIDTH], BF16, name="bank_sb")
+                nc.sync.dma_start(out=bank_sb[:], in_=mem_view[b, k])
+                banks.append(bank_sb)
+            return banks
+
+        def load_chunk(g):
+            b, c = divmod(g, N_CHUNKS // SAMPLES)
+            pre_sb = pre_pool.tile([P, PACK, WIDTH], BF16, name="pre_sb")
+            nc.sync.dma_start(out=pre_sb[:], in_=pre_view[b, :, PACK * c : PACK * (c + 1), :])
+            return pre_sb
+
+        def load_projection():
+            nc.sync.dma_start(
+                out=w_codes[:].bitcast(I32),
+                in_=proj_out_w_words[0].rearrange("p n t -> p (n t)").bitcast(I32),
+            )
+            for q in range(4):
+                nc.sync.dma_start(
+                    out=w_scales[32 * q : 32 * q + 4, :].bitcast(I32),
+                    in_=proj_out_w_scales[0, 4 * q : 4 * q + 4, :].bitcast(I32),
+                )
+            nc.sync.dma_start(out=bias_rows[0:1, :], in_=proj_out_b.rearrange("(o n) -> o n", o=1))
+
+        w_sum, w_t, w_grouped = {}, {}, {}
+
+        def sum_memory(b, banks, acc_psum):
+            pair_sum = sum_pool.tile([P, PACK, WIDTH], F32, name="pair_sum")
+            nc.vector.tensor_tensor(out=pair_sum[:], in0=banks[0][:], in1=banks[1][:], op=ADD)
+            accs = [acc_psum.tile([P, WIDTH], F32, name="acc") for j in range(PACK)]
+            for k in range(VECTOR_BANKS, BANKS):
+                for j in range(PACK):
+                    nc.tensor.matmul(
+                        out=accs[j][:],
+                        lhsT=ident_bf[:],
+                        rhs=banks[k][:, j, :],
+                        start=(k == VECTOR_BANKS),
+                        stop=(k == BANKS - 1),
+                    )
+            for j in range(PACK):
+                w_sum[b, j] = quarter_pool.tile([P, PACK, P], BF16, name="w_sum")
+                nc.vector.tensor_tensor(
+                    out=w_sum[b, j][:],
+                    in0=accs[j][:].rearrange("p (q t) -> p t q", t=PACK),
+                    in1=pair_sum[:, j, :].rearrange("p (q t) -> p t q", t=PACK),
+                    op=ADD,
+                )
+
+        def transpose_quarter(b, j):
+            if not 0 <= j < PACK:
+                return
+            w_t[b, j] = tp_psum.tile([P, PACK, P], BF16, name="tp_bank")
+            for t in range(PACK):
+                nc.tensor.transpose(w_t[b, j][:, t, :], w_sum[b, j][:, t, :], ident_bf[:])
+
+        def regroup_quarter(b, j):
+            if not 0 <= j < PACK:
+                return
+            w_grouped[b, j] = quarter_pool.tile([P, P, PACK], BF16, align_bytes=64, name="w_grouped")
+            nc.scalar.copy(out=w_grouped[b, j][:], in_=w_t[b, j][:].rearrange("q t c -> q c t"))
+
+        def quantise_quarter(b, j):
+            if not 0 <= j < PACK:
+                return
+            cols = slice(j * P, (j + 1) * P)
+            nc.vector.quantize_mx(
+                out=mem_codes[b][:, cols].bitcast(FP8X4),
+                scales=mem_scales[b][:, cols],
+                in_=w_grouped[b, j][:].rearrange("q c t -> q (c t)"),
+            )
+
+        def spread_bias():
+            bias_bank = tp_psum.tile([P, WIDTH], F32, name="tp_bank")
+            nc.tensor.matmul(out=bias_bank[:], lhsT=ones[:], rhs=bias_rows[:], start=True, stop=True)
+            nc.vector.tensor_copy(out=bias_all[:], in_=bias_bank[:])
+
+        pre_sb = {}
+        banks0 = load_memory(0)
+        with tc.psum_pool(name="acc", bufs=PACK) as acc_psum:
+            sum_memory(0, banks0, acc_psum)
+            for j in range(PACK):
+                transpose_quarter(0, j)
+                regroup_quarter(0, j)
+            for j in range(PACK):
+                quantise_quarter(0, j)
+            banks1 = load_memory(1)
+            pre_sb[0] = load_chunk(0)
+            load_projection()
+            for g in range(1, N_CHUNKS):
+                pre_sb[g] = load_chunk(g)
+            sum_memory(1, banks1, acc_psum)
+            for j in range(PACK):
+                transpose_quarter(1, j)
+                regroup_quarter(1, j)
+            for j in range(PACK):
+                quantise_quarter(1, j)
+        spread_bias()
+
+        post_psum = ctx.enter_context(tc.psum_pool(name="post", bufs=3, reuse_waits="tile"))
+        out_psum = ctx.enter_context(tc.psum_pool(name="outp", bufs=3, reuse_waits="tile"))
+
+        tp_banks, pre_grouped, pre_codes, pre_scales = {}, {}, {}, {}
+
+        def transpose_chunk(g):
+            if not 0 <= g < N_CHUNKS:
+                return
+            words = pre_sb[g][:].bitcast(F32)
+            for h in range(2):
+                tp_banks[g, h] = tp_psum.tile([P, 2, 2, P], F32, name="tp_bank")
+                for a in range(2):
+                    for u in range(2):
+                        nc.tensor.transpose(
+                            tp_banks[g, h][:, a, u, :],
+                            words[:, 2 * h + a, u : 2 * P : 2],
+                            ident_f32[:],
+                        )
+
+        def regroup_chunk(g):
+            if not 0 <= g < N_CHUNKS:
+                return
+            pre_grouped[g] = chunk_pool.tile([P, PACK, P, PACK], BF16, align_bytes=64, name="pre_grouped")
+            for h in range(2):
+                nc.scalar.copy(
+                    out=pre_grouped[g][:, 2 * h : 2 * h + 2, :, :].bitcast(F32),
+                    in_=tp_banks[g, h][:].rearrange("q a u c -> q a c u"),
+                )
+
+        def quantise_chunk(g):
+            if not 0 <= g < N_CHUNKS:
+                return
+            pre_codes[g] = chunk_pool.tile([P, PACK * P], U32, align_bytes=64, name="pre_codes")
+            pre_scales[g] = chunk_pool.tile([P, PACK * P], U8, align_bytes=64, name="pre_scales")
+            nc.vector.quantize_mx(
+                out=pre_codes[g][:].bitcast(FP8X4),
+                scales=pre_scales[g][:],
+                in_=pre_grouped[g][:].rearrange("q r c t -> q (r c t)"),
+            )
+
+        post_banks, post_grouped, post_codes, post_scales, out_banks = {}, {}, {}, {}, {}
+
+        def first_matmul(n):
+            if not 0 <= n < N_TILES:
+                return
+            g, r = divmod(n, PACK)
+            b = g // (N_CHUNKS // SAMPLES)
+            toks = slice(r * P, (r + 1) * P)
+            post_banks[n] = post_psum.tile([P, PACK, P], F32, name="post_bank")
+            for j in range(PACK):
+                cols = slice(j * P, (j + 1) * P)
+                nc.tensor.matmul_mx(
+                    out=post_banks[n][:, j, :],
+                    lhsT=mem_codes[b][:, cols].bitcast(FP8X4),
+                    lhsT_scale=mem_scales[b][:, cols],
+                    rhs=pre_codes[g][:, toks].bitcast(FP8X4),
+                    rhs_scale=pre_scales[g][:, toks],
+                    start=True,
+                    stop=True,
+                )
+
+        def regroup_post(n):
+            if not 0 <= n < N_TILES:
+                return
+            m, half = divmod(n, PAIR)
+            if half == 0:
+                post_grouped[m] = pair_pool.tile([P, PAIR, P, PACK], BF16, align_bytes=64, name="post_grouped")
+            nc.scalar.copy(
+                out=post_grouped[m][:, half, :, :], in_=post_banks[n][:].rearrange("p j c -> p c j")
+            )
+
+        def quantise_post(n):
+            if not 0 <= n < N_TILES or n % PAIR != PAIR - 1:
+                return
+            m = n // PAIR
+            post_codes[m] = pair_pool.tile([P, PAIR * P], U32, align_bytes=64, name="post_codes")
+            post_scales[m] = pair_pool.tile([P, PAIR * P], U8, align_bytes=64, name="post_scales")
+            nc.vector.quantize_mx(
+                out=post_codes[m][:].bitcast(FP8X4),
+                scales=post_scales[m][:],
+                in_=post_grouped[m][:].rearrange("p h c j -> p (h c j)"),
+            )
+
+        def second_matmul(n):
+            if not 0 <= n < N_TILES:
+                return
+            m, half = divmod(n, PAIR)
+            toks = slice(half * P, (half + 1) * P)
+            out_banks[n] = out_psum.tile([P, WIDTH], F32, name="out_bank")
+            nc.tensor.matmul_mx(
+                out=out_banks[n][:],
+                lhsT=post_codes[m][:, toks].bitcast(FP8X4),
+                lhsT_scale=post_scales[m][:, toks],
+                rhs=w_codes[:].bitcast(FP8X4),
+                rhs_scale=w_scales[:],
+                start=True,
+                stop=True,
+            )
+
+        def add_bias_and_store(n):
+            if not 0 <= n < N_TILES:
+                return
+            b, s = divmod(n, N_TILES // SAMPLES)
+            out_sb = store_pool.tile([P, WIDTH], F32, name="out_sb")
+            nc.vector.tensor_tensor(out=out_sb[:], in0=out_banks[n][:], in1=bias_all[:], op=ADD)
+            nc.sync.dma_start(out=out_view[b, :, s, :], in_=out_sb[:])
+
+        for g in range(-TRANSPOSE_AHEAD, N_CHUNKS):
+            regroup_chunk(g + REGROUP_PRE_AHEAD)
+            quantise_chunk(g + QUANTISE_PRE_AHEAD)
+            for r in range(PACK):
+                n = PACK * g + r
+                if r == TRANSPOSE_BEFORE_TILE:
+                    transpose_chunk(g + TRANSPOSE_AHEAD)
+                second_matmul(n + SECOND_MATMUL_AHEAD)
+                first_matmul(n + FIRST_MATMUL_AHEAD)
+                regroup_post(n + REGROUP_POST_AHEAD)
+                add_bias_and_store(n)
+                quantise_post(n + QUANTISE_POST_AHEAD)

@@ -10,6 +10,7 @@ U32 = mybir.dt.uint32
 U8 = mybir.dt.uint8
 FP8X4 = mybir.dt.float8_e4m3fn_x4
 ADD = mybir.AluOpType.add
+AXIS_X = mybir.AxisListType.X
 
 P = 128
 PACK = 4
@@ -17,7 +18,9 @@ SAMPLES = 2
 TOKENS = 4096
 WIDTH = 512
 BANKS = 8
-VECTOR_BANKS = 2
+ROWS = WIDTH // (P // BANKS)
+PIECES = 4
+EDGE = P // BANKS
 N_CHUNKS = SAMPLES * TOKENS // (PACK * P)
 N_TILES = N_CHUNKS * PACK
 PAIR = 2
@@ -31,6 +34,10 @@ REGROUP_POST_AHEAD = 8
 QUANTISE_POST_AHEAD = 5
 SECOND_MATMUL_AHEAD = 3
 
+HEAD_CHUNKS = 1
+MEMORY_1_AFTER_CHUNK = 5
+MEMORY_1_TILES = {(3, 0): 0, (3, 2): 1, (4, 0): 2, (4, 2): 3}
+
 FLOPS = 2 * 2 * SAMPLES * TOKENS * WIDTH * WIDTH
 
 
@@ -40,24 +47,27 @@ def tile_proceduralmemory_pc_t_kernel(
     nc = tc.nc
     pre_view = pre.rearrange("b (p s) i -> b p s i", p=P)
     out_view = out.rearrange("b (p s) n -> b p s n", p=P)
-    mem_view = W_pm.rearrange("b k (p j) i -> b k p j i", j=PACK)
+    mem_view = W_pm.rearrange("b k o i -> b (k o i)").rearrange("b (p s i) -> b p s i", p=P, i=WIDTH)
 
     with ExitStack() as ctx:
         ctx.enter_context(tc.manual_schedule())
         const = ctx.enter_context(tc.tile_pool(name="const", bufs=1))
-        mem_pool = ctx.enter_context(tc.tile_pool(name="mem", bufs=BANKS))
+        mem_pool = ctx.enter_context(tc.tile_pool(name="mem", bufs=PIECES))
         pre_pool = ctx.enter_context(tc.tile_pool(name="pre", bufs=N_CHUNKS))
-        sum_pool = ctx.enter_context(tc.tile_pool(name="sum", bufs=2))
         quarter_pool = ctx.enter_context(tc.tile_pool(name="quarter", bufs=PACK))
         chunk_pool = ctx.enter_context(tc.tile_pool(name="chunk", bufs=4))
         pair_pool = ctx.enter_context(tc.tile_pool(name="pair", bufs=4))
-        store_pool = ctx.enter_context(tc.tile_pool(name="store", bufs=24))
+        store_pool = ctx.enter_context(tc.tile_pool(name="store", bufs=12))
         tp_psum = ctx.enter_context(tc.psum_pool(name="tp", bufs=2))
 
         ident_f32 = const.tile([P, P], F32)
         make_identity(nc, ident_f32[:])
-        ident_bf = const.tile([P, P], BF16)
-        make_identity(nc, ident_bf[:])
+        adder_f32 = const.tile([P, EDGE], F32)
+        nc.vector.tensor_reduce(
+            out=adder_f32[:], in_=ident_f32[:].rearrange("p (k e) -> p e k", e=EDGE), axis=AXIS_X, op=ADD
+        )
+        adder = const.tile([P, EDGE], BF16)
+        nc.vector.tensor_copy(out=adder[:], in_=adder_f32[:])
         ones = const.tile([P, P], BF16)
         nc.vector.memset(ones[:], 1.0)
         bias_rows = const.tile([P, WIDTH], BF16)
@@ -74,12 +84,13 @@ def tile_proceduralmemory_pc_t_kernel(
         ]
 
         def load_memory(b):
-            banks = []
-            for k in range(BANKS):
-                bank_sb = mem_pool.tile([P, PACK, WIDTH], BF16, name="bank_sb")
-                nc.sync.dma_start(out=bank_sb[:], in_=mem_view[b, k])
-                banks.append(bank_sb)
-            return banks
+            pieces = []
+            n_rows = ROWS // PIECES
+            for c in range(PIECES):
+                piece = mem_pool.tile([P, n_rows, WIDTH], BF16, name="mem_piece")
+                nc.sync.dma_start(out=piece[:], in_=mem_view[b, :, c * n_rows : (c + 1) * n_rows, :])
+                pieces.append(piece)
+            return pieces
 
         def load_chunk(g):
             b, c = divmod(g, N_CHUNKS // SAMPLES)
@@ -99,46 +110,27 @@ def tile_proceduralmemory_pc_t_kernel(
                 )
             nc.sync.dma_start(out=bias_rows[0:1, :], in_=proj_out_b.rearrange("(o n) -> o n", o=1))
 
-        w_sum, w_t, w_grouped = {}, {}, {}
+        w_grouped = {}
 
-        def sum_memory(b, banks, acc_psum):
-            pair_sum = sum_pool.tile([P, PACK, WIDTH], F32, name="pair_sum")
-            nc.vector.tensor_tensor(out=pair_sum[:], in0=banks[0][:], in1=banks[1][:], op=ADD)
-            accs = [acc_psum.tile([P, WIDTH], F32, name="acc") for j in range(PACK)]
-            for k in range(VECTOR_BANKS, BANKS):
-                for j in range(PACK):
-                    nc.tensor.matmul(
-                        out=accs[j][:],
-                        lhsT=ident_bf[:],
-                        rhs=banks[k][:, j, :],
-                        start=(k == VECTOR_BANKS),
-                        stop=(k == BANKS - 1),
-                    )
-            for j in range(PACK):
-                w_sum[b, j] = quarter_pool.tile([P, PACK, P], BF16, name="w_sum")
-                nc.vector.tensor_tensor(
-                    out=w_sum[b, j][:],
-                    in0=accs[j][:].rearrange("p (q t) -> p t q", t=PACK),
-                    in1=pair_sum[:, j, :].rearrange("p (q t) -> p t q", t=PACK),
-                    op=ADD,
+        def sum_row(pieces, s, bank):
+            c, row = divmod(s, ROWS // PIECES)
+            for t in range(PACK):
+                nc.tensor.matmul(
+                    out=bank[:, t, s // PACK, :],
+                    lhsT=pieces[c][:, row, t::PACK],
+                    rhs=adder[:],
+                    start=True,
+                    stop=True,
                 )
 
-        def transpose_quarter(b, j):
-            if not 0 <= j < PACK:
-                return
-            w_t[b, j] = tp_psum.tile([P, PACK, P], BF16, name="tp_bank")
-            for t in range(PACK):
-                nc.tensor.transpose(w_t[b, j][:, t, :], w_sum[b, j][:, t, :], ident_bf[:])
-
-        def regroup_quarter(b, j):
-            if not 0 <= j < PACK:
-                return
+        def regroup_quarter(b, j, bank, copy):
             w_grouped[b, j] = quarter_pool.tile([P, P, PACK], BF16, align_bytes=64, name="w_grouped")
-            nc.scalar.copy(out=w_grouped[b, j][:], in_=w_t[b, j][:].rearrange("q t c -> q c t"))
+            copy(
+                out=w_grouped[b, j][:].rearrange("q (e s) t -> q e s t", s=ROWS // PACK),
+                in_=bank[:].rearrange("q t s e -> q e s t"),
+            )
 
         def quantise_quarter(b, j):
-            if not 0 <= j < PACK:
-                return
             cols = slice(j * P, (j + 1) * P)
             nc.vector.quantize_mx(
                 out=mem_codes[b][:, cols].bitcast(FP8X4),
@@ -146,35 +138,52 @@ def tile_proceduralmemory_pc_t_kernel(
                 in_=w_grouped[b, j][:].rearrange("q c t -> q (c t)"),
             )
 
+        def prepare_memory_0(pieces):
+            banks = []
+            for j in range(PACK):
+                pool, name = (post_psum, "post_bank") if j < 2 else (out_psum, "out_bank")
+                banks.append(pool.tile([P, PACK, ROWS // PACK, EDGE], F32, name=name))
+            for s in range(ROWS):
+                sum_row(pieces, s, banks[s % PACK])
+            for j in range(PACK):
+                regroup_quarter(0, j, banks[j], nc.scalar.copy if j % 2 == 0 else nc.vector.tensor_copy)
+            for j in range(PACK):
+                quantise_quarter(0, j)
+
+        mem1_banks = {}
+
+        def memory_1_stage(step, r):
+            n = PACK * step + r
+            at = {PACK * g + q: j for (g, q), j in MEMORY_1_TILES.items()}
+            if n - 2 in at:
+                quantise_quarter(1, at[n - 2])
+            if n - 1 in at:
+                j = at[n - 1]
+                regroup_quarter(1, j, mem1_banks[j], nc.scalar.copy if j % 2 == 0 else nc.vector.tensor_copy)
+            if n in at:
+                j = at[n]
+                mem1_banks[j] = post_psum.tile([P, PACK, ROWS // PACK, EDGE], F32, name="post_bank")
+                for s in range(j, ROWS, PACK):
+                    sum_row(mem_pieces[1], s, mem1_banks[j])
+
         def spread_bias():
             bias_bank = tp_psum.tile([P, WIDTH], F32, name="tp_bank")
             nc.tensor.matmul(out=bias_bank[:], lhsT=ones[:], rhs=bias_rows[:], start=True, stop=True)
             nc.vector.tensor_copy(out=bias_all[:], in_=bias_bank[:])
 
-        pre_sb = {}
-        banks0 = load_memory(0)
-        with tc.psum_pool(name="acc", bufs=PACK) as acc_psum:
-            sum_memory(0, banks0, acc_psum)
-            for j in range(PACK):
-                transpose_quarter(0, j)
-                regroup_quarter(0, j)
-            for j in range(PACK):
-                quantise_quarter(0, j)
-            banks1 = load_memory(1)
-            pre_sb[0] = load_chunk(0)
-            load_projection()
-            for g in range(1, N_CHUNKS):
-                pre_sb[g] = load_chunk(g)
-            sum_memory(1, banks1, acc_psum)
-            for j in range(PACK):
-                transpose_quarter(1, j)
-                regroup_quarter(1, j)
-            for j in range(PACK):
-                quantise_quarter(1, j)
-        spread_bias()
+        post_psum = ctx.enter_context(tc.psum_pool(name="post", bufs=3))
+        out_psum = ctx.enter_context(tc.psum_pool(name="outp", bufs=3))
 
-        post_psum = ctx.enter_context(tc.psum_pool(name="post", bufs=3, reuse_waits="tile"))
-        out_psum = ctx.enter_context(tc.psum_pool(name="outp", bufs=3, reuse_waits="tile"))
+        pre_sb, mem_pieces = {}, {}
+        for g in range(HEAD_CHUNKS):
+            pre_sb[g] = load_chunk(g)
+        mem_pieces[0] = load_memory(0)
+        for g in range(HEAD_CHUNKS, N_CHUNKS):
+            pre_sb[g] = load_chunk(g)
+            if g == HEAD_CHUNKS:
+                load_projection()
+            if g == MEMORY_1_AFTER_CHUNK:
+                mem_pieces[1] = load_memory(1)
 
         tp_banks, pre_grouped, pre_codes, pre_scales = {}, {}, {}, {}
 
@@ -213,7 +222,8 @@ def tile_proceduralmemory_pc_t_kernel(
                 in_=pre_grouped[g][:].rearrange("q r c t -> q (r c t)"),
             )
 
-        post_banks, post_grouped, post_codes, post_scales, out_banks = {}, {}, {}, {}, {}
+        post_banks, post_grouped, post_codes, post_scales = {}, {}, {}, {}
+        out_banks, out_rows = {}, {}
 
         def first_matmul(n):
             if not 0 <= n < N_TILES:
@@ -275,20 +285,33 @@ def tile_proceduralmemory_pc_t_kernel(
         def add_bias_and_store(n):
             if not 0 <= n < N_TILES:
                 return
-            b, s = divmod(n, N_TILES // SAMPLES)
-            out_sb = store_pool.tile([P, WIDTH], F32, name="out_sb")
-            nc.vector.tensor_tensor(out=out_sb[:], in0=out_banks[n][:], in1=bias_all[:], op=ADD)
-            nc.sync.dma_start(out=out_view[b, :, s, :], in_=out_sb[:])
+            m, half = divmod(n, PAIR)
+            if half == 0:
+                out_rows[m] = store_pool.tile([P, PAIR, WIDTH], F32, name="out_rows")
+            nc.vector.tensor_tensor(out=out_rows[m][:, half, :], in0=out_banks[n][:], in1=bias_all[:], op=ADD)
+            if half == PAIR - 1:
+                b, s = divmod(PAIR * m, N_TILES // SAMPLES)
+                nc.sync.dma_start(out=out_view[b, :, s : s + PAIR, :], in_=out_rows[m][:])
 
-        for g in range(-TRANSPOSE_AHEAD, N_CHUNKS):
-            regroup_chunk(g + REGROUP_PRE_AHEAD)
-            quantise_chunk(g + QUANTISE_PRE_AHEAD)
+        for g in range(HEAD_CHUNKS):
+            transpose_chunk(g)
+            regroup_chunk(g)
+            quantise_chunk(g)
+        prepare_memory_0(mem_pieces[0])
+        for g in range(HEAD_CHUNKS - TRANSPOSE_AHEAD, N_CHUNKS):
+            if g + REGROUP_PRE_AHEAD >= HEAD_CHUNKS:
+                regroup_chunk(g + REGROUP_PRE_AHEAD)
+            if g + QUANTISE_PRE_AHEAD >= HEAD_CHUNKS:
+                quantise_chunk(g + QUANTISE_PRE_AHEAD)
+            if g == 0:
+                spread_bias()
             for r in range(PACK):
                 n = PACK * g + r
                 if r == TRANSPOSE_BEFORE_TILE:
                     transpose_chunk(g + TRANSPOSE_AHEAD)
                 second_matmul(n + SECOND_MATMUL_AHEAD)
                 first_matmul(n + FIRST_MATMUL_AHEAD)
+                memory_1_stage(g, r)
                 regroup_post(n + REGROUP_POST_AHEAD)
                 add_bias_and_store(n)
                 quantise_post(n + QUANTISE_POST_AHEAD)

@@ -25,18 +25,21 @@ N_CHUNKS = SAMPLES * TOKENS // (PACK * P)
 N_TILES = N_CHUNKS * PACK
 PAIR = 2
 
-TRANSPOSE_AHEAD = 5
-REGROUP_PRE_AHEAD = 4
-QUANTISE_PRE_AHEAD = 3
-TRANSPOSE_BEFORE_TILE = 3
-FIRST_MATMUL_AHEAD = 9
-REGROUP_POST_AHEAD = 8
-QUANTISE_POST_AHEAD = 5
-SECOND_MATMUL_AHEAD = 3
+TRANSPOSE_LEAD = 15
+REGROUP_PRE_LEAD = 13
+QUANTISE_PRE_LEAD = 10
+FIRST_MATMUL_LEAD = 9
+REGROUP_POST_LEAD = 8
+QUANTISE_POST_LEAD = 5
+SECOND_MATMUL_LEAD = 2
 
 HEAD_CHUNKS = 1
 MEMORY_1_AFTER_CHUNK = 5
-MEMORY_1_TILES = {(3, 0): 0, (3, 2): 1, (4, 0): 2, (4, 2): 3}
+MEMORY_1_START = 11
+MEMORY_1_ROWS = 4
+MEMORY_1_COPY_LAG = 1
+MEMORY_1_QUANTISE_LAG = 4
+TP_BANKS, POST_BANKS, OUT_BANKS = 2, 3, 3
 
 FLOPS = 2 * 2 * SAMPLES * TOKENS * WIDTH * WIDTH
 
@@ -57,8 +60,8 @@ def tile_proceduralmemory_pc_t_kernel(
         quarter_pool = ctx.enter_context(tc.tile_pool(name="quarter", bufs=PACK))
         chunk_pool = ctx.enter_context(tc.tile_pool(name="chunk", bufs=4))
         pair_pool = ctx.enter_context(tc.tile_pool(name="pair", bufs=4))
-        store_pool = ctx.enter_context(tc.tile_pool(name="store", bufs=12))
-        tp_psum = ctx.enter_context(tc.psum_pool(name="tp", bufs=2))
+        store_pool = ctx.enter_context(tc.tile_pool(name="store", bufs=16))
+        tp_psum = ctx.enter_context(tc.psum_pool(name="tp", bufs=TP_BANKS))
 
         ident_f32 = const.tile([P, P], F32)
         make_identity(nc, ident_f32[:])
@@ -108,7 +111,6 @@ def tile_proceduralmemory_pc_t_kernel(
                     out=w_scales[32 * q : 32 * q + 4, :].bitcast(I32),
                     in_=proj_out_w_scales[0, 4 * q : 4 * q + 4, :].bitcast(I32),
                 )
-            nc.sync.dma_start(out=bias_rows[0:1, :], in_=proj_out_b.rearrange("(o n) -> o n", o=1))
 
         w_grouped = {}
 
@@ -152,29 +154,30 @@ def tile_proceduralmemory_pc_t_kernel(
 
         mem1_banks = {}
 
-        def memory_1_stage(step, r):
-            n = PACK * step + r
-            at = {PACK * g + q: j for (g, q), j in MEMORY_1_TILES.items()}
-            if n - 2 in at:
-                quantise_quarter(1, at[n - 2])
-            if n - 1 in at:
-                j = at[n - 1]
-                regroup_quarter(1, j, mem1_banks[j], nc.scalar.copy if j % 2 == 0 else nc.vector.tensor_copy)
-            if n in at:
-                j = at[n]
-                mem1_banks[j] = post_psum.tile([P, PACK, ROWS // PACK, EDGE], F32, name="post_bank")
-                for s in range(j, ROWS, PACK):
-                    sum_row(mem_pieces[1], s, mem1_banks[j])
+        def memory_1_turn(n):
+            per = ROWS // PACK // MEMORY_1_ROWS
+            for j in range(PACK):
+                first = MEMORY_1_START + j * per
+                if n == first + per - 1 + MEMORY_1_QUANTISE_LAG:
+                    quantise_quarter(1, j)
+                if n == first + per - 1 + MEMORY_1_COPY_LAG:
+                    regroup_quarter(1, j, mem1_banks[j], nc.scalar.copy)
+                if first <= n < first + per:
+                    if n == first:
+                        mem1_banks[j] = post_psum.tile([P, PACK, ROWS // PACK, EDGE], F32, name="post_bank")
+                    for row in range((n - first) * MEMORY_1_ROWS, (n - first + 1) * MEMORY_1_ROWS):
+                        sum_row(mem_pieces[1], PACK * row + j, mem1_banks[j])
 
         def spread_bias():
-            bias_bank = tp_psum.tile([P, WIDTH], F32, name="tp_bank")
+            bias_bank = out_psum.tile([P, WIDTH], F32, name="out_bank")
             nc.tensor.matmul(out=bias_bank[:], lhsT=ones[:], rhs=bias_rows[:], start=True, stop=True)
             nc.vector.tensor_copy(out=bias_all[:], in_=bias_bank[:])
 
-        post_psum = ctx.enter_context(tc.psum_pool(name="post", bufs=3))
-        out_psum = ctx.enter_context(tc.psum_pool(name="outp", bufs=3))
+        post_psum = ctx.enter_context(tc.psum_pool(name="post", bufs=POST_BANKS))
+        out_psum = ctx.enter_context(tc.psum_pool(name="outp", bufs=OUT_BANKS))
 
         pre_sb, mem_pieces = {}, {}
+        nc.sync.dma_start(out=bias_rows[0:1, :], in_=proj_out_b.rearrange("(o n) -> o n", o=1))
         for g in range(HEAD_CHUNKS):
             pre_sb[g] = load_chunk(g)
         mem_pieces[0] = load_memory(0)
@@ -297,21 +300,20 @@ def tile_proceduralmemory_pc_t_kernel(
             transpose_chunk(g)
             regroup_chunk(g)
             quantise_chunk(g)
+        spread_bias()
         prepare_memory_0(mem_pieces[0])
-        for g in range(HEAD_CHUNKS - TRANSPOSE_AHEAD, N_CHUNKS):
-            if g + REGROUP_PRE_AHEAD >= HEAD_CHUNKS:
-                regroup_chunk(g + REGROUP_PRE_AHEAD)
-            if g + QUANTISE_PRE_AHEAD >= HEAD_CHUNKS:
-                quantise_chunk(g + QUANTISE_PRE_AHEAD)
-            if g == 0:
-                spread_bias()
-            for r in range(PACK):
-                n = PACK * g + r
-                if r == TRANSPOSE_BEFORE_TILE:
-                    transpose_chunk(g + TRANSPOSE_AHEAD)
-                second_matmul(n + SECOND_MATMUL_AHEAD)
-                first_matmul(n + FIRST_MATMUL_AHEAD)
-                memory_1_stage(g, r)
-                regroup_post(n + REGROUP_POST_AHEAD)
-                add_bias_and_store(n)
-                quantise_post(n + QUANTISE_POST_AHEAD)
+
+        def chunk_at(n):
+            g, r = divmod(n, PACK)
+            return g if r == 0 and g >= HEAD_CHUNKS else -1
+
+        for n in range(min(PACK * HEAD_CHUNKS - TRANSPOSE_LEAD, -FIRST_MATMUL_LEAD), N_TILES):
+            regroup_chunk(chunk_at(n + REGROUP_PRE_LEAD))
+            quantise_chunk(chunk_at(n + QUANTISE_PRE_LEAD))
+            second_matmul(n + SECOND_MATMUL_LEAD)
+            first_matmul(n + FIRST_MATMUL_LEAD)
+            transpose_chunk(chunk_at(n + TRANSPOSE_LEAD))
+            memory_1_turn(n)
+            regroup_post(n + REGROUP_POST_LEAD)
+            add_bias_and_store(n)
+            quantise_post(n + QUANTISE_POST_LEAD)

@@ -19,7 +19,8 @@ TOKENS = 4096
 WIDTH = 512
 BANKS = 8
 ROWS = WIDTH // (P // BANKS)
-PIECES = 4
+PIECE_ROWS = (8, 8, 8, 4, 4)
+EARLY_ROWS = 24
 EDGE = P // BANKS
 N_CHUNKS = SAMPLES * TOKENS // (PACK * P)
 N_TILES = N_CHUNKS * PACK
@@ -55,14 +56,16 @@ def tile_proceduralmemory_pc_t_kernel(
     with ExitStack() as ctx:
         ctx.enter_context(tc.manual_schedule())
         const = ctx.enter_context(tc.tile_pool(name="const", bufs=1))
-        mem_pool = ctx.enter_context(tc.tile_pool(name="mem", bufs=PIECES))
+        mem_pool = ctx.enter_context(tc.tile_pool(name="mem", bufs=len(PIECE_ROWS)))
         pre_pool = ctx.enter_context(tc.tile_pool(name="pre", bufs=N_CHUNKS))
         quarter_pool = ctx.enter_context(tc.tile_pool(name="quarter", bufs=PACK))
         chunk_pool = ctx.enter_context(tc.tile_pool(name="chunk", bufs=4))
         pair_pool = ctx.enter_context(tc.tile_pool(name="pair", bufs=4))
-        store_pool = ctx.enter_context(tc.tile_pool(name="store", bufs=16))
+        store_pool = ctx.enter_context(tc.tile_pool(name="store", bufs=14))
         tp_psum = ctx.enter_context(tc.psum_pool(name="tp", bufs=TP_BANKS))
 
+        bias_rows = const.tile([P, WIDTH], BF16)
+        nc.vector.memset(bias_rows[:], 0.0)
         ident_f32 = const.tile([P, P], F32)
         make_identity(nc, ident_f32[:])
         adder_f32 = const.tile([P, EDGE], F32)
@@ -73,8 +76,6 @@ def tile_proceduralmemory_pc_t_kernel(
         nc.vector.tensor_copy(out=adder[:], in_=adder_f32[:])
         ones = const.tile([P, P], BF16)
         nc.vector.memset(ones[:], 1.0)
-        bias_rows = const.tile([P, WIDTH], BF16)
-        nc.vector.memset(bias_rows[:], 0.0)
         w_scales = const.tile([P, WIDTH], U8, align_bytes=64)
         nc.vector.memset(w_scales[:].bitcast(I32), 0)
         w_codes = const.tile([P, WIDTH], U32, align_bytes=64)
@@ -87,13 +88,12 @@ def tile_proceduralmemory_pc_t_kernel(
         ]
 
         def load_memory(b):
-            pieces = []
-            n_rows = ROWS // PIECES
-            for c in range(PIECES):
-                piece = mem_pool.tile([P, n_rows, WIDTH], BF16, name="mem_piece")
-                nc.sync.dma_start(out=piece[:], in_=mem_view[b, :, c * n_rows : (c + 1) * n_rows, :])
-                pieces.append(piece)
-            return pieces
+            rows = []
+            for n_rows in PIECE_ROWS:
+                piece = mem_pool.tile([P, max(PIECE_ROWS), WIDTH], BF16, name="mem_piece")
+                nc.sync.dma_start(out=piece[:, :n_rows, :], in_=mem_view[b, :, len(rows) : len(rows) + n_rows, :])
+                rows.extend(piece[:, r, :] for r in range(n_rows))
+            return rows
 
         def load_chunk(g):
             b, c = divmod(g, N_CHUNKS // SAMPLES)
@@ -114,22 +114,19 @@ def tile_proceduralmemory_pc_t_kernel(
 
         w_grouped = {}
 
-        def sum_row(pieces, s, bank):
-            c, row = divmod(s, ROWS // PIECES)
+        def sum_row(rows, s, bank, at):
             for t in range(PACK):
                 nc.tensor.matmul(
-                    out=bank[:, t, s // PACK, :],
-                    lhsT=pieces[c][:, row, t::PACK],
-                    rhs=adder[:],
-                    start=True,
-                    stop=True,
+                    out=bank[:, t, at, :], lhsT=rows[s][:, t::PACK], rhs=adder[:], start=True, stop=True
                 )
 
-        def regroup_quarter(b, j, bank, copy):
+        def new_quarter(b, j):
             w_grouped[b, j] = quarter_pool.tile([P, P, PACK], BF16, align_bytes=64, name="w_grouped")
+
+        def regroup_quarter(b, j, bank, first, count, copy):
             copy(
-                out=w_grouped[b, j][:].rearrange("q (e s) t -> q e s t", s=ROWS // PACK),
-                in_=bank[:].rearrange("q t s e -> q e s t"),
+                out=w_grouped[b, j][:].rearrange("q (e s) t -> q e s t", s=ROWS // PACK)[:, :, first : first + count, :],
+                in_=bank[:, :, :count, :].rearrange("q t s e -> q e s t"),
             )
 
         def quantise_quarter(b, j):
@@ -140,15 +137,20 @@ def tile_proceduralmemory_pc_t_kernel(
                 in_=w_grouped[b, j][:].rearrange("q c t -> q (c t)"),
             )
 
-        def prepare_memory_0(pieces):
-            banks = []
+        def prepare_memory_0(rows):
             for j in range(PACK):
-                pool, name = (post_psum, "post_bank") if j < 2 else (out_psum, "out_bank")
-                banks.append(pool.tile([P, PACK, ROWS // PACK, EDGE], F32, name=name))
-            for s in range(ROWS):
-                sum_row(pieces, s, banks[s % PACK])
-            for j in range(PACK):
-                regroup_quarter(0, j, banks[j], nc.scalar.copy if j % 2 == 0 else nc.vector.tensor_copy)
+                new_quarter(0, j)
+            for lo, hi in ((0, EARLY_ROWS), (EARLY_ROWS, ROWS)):
+                first, count = lo // PACK, (hi - lo) // PACK
+                banks = []
+                for j in range(PACK):
+                    pool, name = (post_psum, "post_bank") if j < 2 else (out_psum, "out_bank")
+                    banks.append(pool.tile([P, PACK, ROWS // PACK, EDGE], F32, name=name))
+                for s in range(lo, hi):
+                    sum_row(rows, s, banks[s % PACK], s // PACK - first)
+                for j in range(PACK):
+                    copy = nc.scalar.copy if j % 2 == 0 else nc.vector.tensor_copy
+                    regroup_quarter(0, j, banks[j], first, count, copy)
             for j in range(PACK):
                 quantise_quarter(0, j)
 
@@ -161,12 +163,13 @@ def tile_proceduralmemory_pc_t_kernel(
                 if n == first + per - 1 + MEMORY_1_QUANTISE_LAG:
                     quantise_quarter(1, j)
                 if n == first + per - 1 + MEMORY_1_COPY_LAG:
-                    regroup_quarter(1, j, mem1_banks[j], nc.scalar.copy)
+                    regroup_quarter(1, j, mem1_banks[j], 0, ROWS // PACK, nc.scalar.copy)
                 if first <= n < first + per:
                     if n == first:
+                        new_quarter(1, j)
                         mem1_banks[j] = post_psum.tile([P, PACK, ROWS // PACK, EDGE], F32, name="post_bank")
                     for row in range((n - first) * MEMORY_1_ROWS, (n - first + 1) * MEMORY_1_ROWS):
-                        sum_row(mem_pieces[1], PACK * row + j, mem1_banks[j])
+                        sum_row(mem_rows[1], PACK * row + j, mem1_banks[j], row)
 
         def spread_bias():
             bias_bank = out_psum.tile([P, WIDTH], F32, name="out_bank")
@@ -176,17 +179,17 @@ def tile_proceduralmemory_pc_t_kernel(
         post_psum = ctx.enter_context(tc.psum_pool(name="post", bufs=POST_BANKS))
         out_psum = ctx.enter_context(tc.psum_pool(name="outp", bufs=OUT_BANKS))
 
-        pre_sb, mem_pieces = {}, {}
-        nc.sync.dma_start(out=bias_rows[0:1, :], in_=proj_out_b.rearrange("(o n) -> o n", o=1))
+        pre_sb, mem_rows = {}, {}
         for g in range(HEAD_CHUNKS):
             pre_sb[g] = load_chunk(g)
-        mem_pieces[0] = load_memory(0)
+        nc.sync.dma_start(out=bias_rows[0:1, :], in_=proj_out_b.rearrange("(o n) -> o n", o=1))
+        mem_rows[0] = load_memory(0)
         for g in range(HEAD_CHUNKS, N_CHUNKS):
             pre_sb[g] = load_chunk(g)
             if g == HEAD_CHUNKS:
                 load_projection()
             if g == MEMORY_1_AFTER_CHUNK:
-                mem_pieces[1] = load_memory(1)
+                mem_rows[1] = load_memory(1)
 
         tp_banks, pre_grouped, pre_codes, pre_scales = {}, {}, {}, {}
 
@@ -292,16 +295,18 @@ def tile_proceduralmemory_pc_t_kernel(
             if half == 0:
                 out_rows[m] = store_pool.tile([P, PAIR, WIDTH], F32, name="out_rows")
             nc.vector.tensor_tensor(out=out_rows[m][:, half, :], in0=out_banks[n][:], in1=bias_all[:], op=ADD)
-            if half == PAIR - 1:
-                b, s = divmod(PAIR * m, N_TILES // SAMPLES)
-                nc.sync.dma_start(out=out_view[b, :, s : s + PAIR, :], in_=out_rows[m][:])
+            b, s = divmod(n, N_TILES // SAMPLES)
+            if n >= N_TILES - PAIR:
+                nc.sync.dma_start(out=out_view[b, :, s, :], in_=out_rows[m][:, half, :])
+            elif half == PAIR - 1:
+                nc.sync.dma_start(out=out_view[b, :, s + 1 - PAIR : s + 1, :], in_=out_rows[m][:])
 
         for g in range(HEAD_CHUNKS):
             transpose_chunk(g)
             regroup_chunk(g)
             quantise_chunk(g)
         spread_bias()
-        prepare_memory_0(mem_pieces[0])
+        prepare_memory_0(mem_rows[0])
 
         def chunk_at(n):
             g, r = divmod(n, PACK)

@@ -26,20 +26,21 @@ N_CHUNKS = SAMPLES * TOKENS // (PACK * P)
 N_TILES = N_CHUNKS * PACK
 PAIR = 2
 
-TRANSPOSE_LEAD = 15
-REGROUP_PRE_LEAD = 13
-QUANTISE_PRE_LEAD = 10
-FIRST_MATMUL_LEAD = 9
-REGROUP_POST_LEAD = 8
-QUANTISE_POST_LEAD = 5
+TRANSPOSE_LEAD = 13
+REGROUP_PRE_LEAD = 11
+QUANTISE_PRE_LEAD = 9
+FIRST_MATMUL_LEAD = 6
+REGROUP_POST_LEAD = 5
+QUANTISE_POST_LEAD = 4
 SECOND_MATMUL_LEAD = 2
 
+VECTOR_CHUNK = 1
 HEAD_CHUNKS = 1
 MEMORY_1_AFTER_CHUNK = 5
-MEMORY_1_START = 11
+MEMORY_1_START = 13
 MEMORY_1_ROWS = 4
 MEMORY_1_COPY_LAG = 1
-MEMORY_1_QUANTISE_LAG = 4
+MEMORY_1_QUANTISE_LAG = 3
 TP_BANKS, POST_BANKS, OUT_BANKS = 2, 3, 3
 
 FLOPS = 2 * 2 * SAMPLES * TOKENS * WIDTH * WIDTH
@@ -212,7 +213,8 @@ def tile_proceduralmemory_pc_t_kernel(
                 return
             pre_grouped[g] = chunk_pool.tile([P, PACK, P, PACK], BF16, align_bytes=64, name="pre_grouped")
             for h in range(2):
-                nc.scalar.copy(
+                copy = nc.vector.tensor_copy if g == VECTOR_CHUNK else nc.scalar.copy
+                copy(
                     out=pre_grouped[g][:, 2 * h : 2 * h + 2, :, :].bitcast(F32),
                     in_=tp_banks[g, h][:].rearrange("q a u c -> q a c u"),
                 )

@@ -62,7 +62,7 @@ def tile_proceduralmemory_pc_t_kernel(
         quarter_pool = ctx.enter_context(tc.tile_pool(name="quarter", bufs=PACK))
         chunk_pool = ctx.enter_context(tc.tile_pool(name="chunk", bufs=4))
         pair_pool = ctx.enter_context(tc.tile_pool(name="pair", bufs=4))
-        store_pool = ctx.enter_context(tc.tile_pool(name="store", bufs=14))
+        store_pool = ctx.enter_context(tc.tile_pool(name="store", bufs=28))
         tp_psum = ctx.enter_context(tc.psum_pool(name="tp", bufs=TP_BANKS))
 
         bias_rows = const.tile([P, WIDTH], BF16)
@@ -231,7 +231,7 @@ def tile_proceduralmemory_pc_t_kernel(
             )
 
         post_banks, post_grouped, post_codes, post_scales = {}, {}, {}, {}
-        out_banks, out_rows = {}, {}
+        out_banks = {}
 
         def first_matmul(n):
             if not 0 <= n < N_TILES:
@@ -293,15 +293,10 @@ def tile_proceduralmemory_pc_t_kernel(
         def add_bias_and_store(n):
             if not 0 <= n < N_TILES:
                 return
-            m, half = divmod(n, PAIR)
-            if half == 0:
-                out_rows[m] = store_pool.tile([P, PAIR, WIDTH], F32, name="out_rows")
-            nc.vector.tensor_tensor(out=out_rows[m][:, half, :], in0=out_banks[n][:], in1=bias_all[:], op=ADD)
             b, s = divmod(n, N_TILES // SAMPLES)
-            if n >= N_TILES - PAIR:
-                nc.sync.dma_start(out=out_view[b, :, s, :], in_=out_rows[m][:, half, :])
-            elif half == PAIR - 1:
-                nc.sync.dma_start(out=out_view[b, :, s + 1 - PAIR : s + 1, :], in_=out_rows[m][:])
+            out_row = store_pool.tile([P, WIDTH], F32, name="out_row")
+            nc.vector.tensor_tensor(out=out_row[:], in0=out_banks[n][:], in1=bias_all[:], op=ADD)
+            nc.sync.dma_start(out=out_view[b, :, s, :], in_=out_row[:])
 
         for g in range(HEAD_CHUNKS):
             transpose_chunk(g)

@@ -90,9 +90,10 @@ def tile_proceduralmemory_pc_t_kernel(
 
         def load_memory(b):
             rows = []
-            for n_rows in PIECE_ROWS:
+            for c, n_rows in enumerate(PIECE_ROWS):
+                queue = nc.scalar if b == 0 and c % 2 == 1 else nc.sync
                 piece = mem_pool.tile([P, max(PIECE_ROWS), WIDTH], BF16, name="mem_piece")
-                nc.sync.dma_start(out=piece[:, :n_rows, :], in_=mem_view[b, :, len(rows) : len(rows) + n_rows, :])
+                queue.dma_start(out=piece[:, :n_rows, :], in_=mem_view[b, :, len(rows) : len(rows) + n_rows, :])
                 rows.extend(piece[:, r, :] for r in range(n_rows))
             return rows
 

from contextlib import ExitStack

import concourse.mybir as mybir
from concourse.masks import make_identity

F32 = mybir.dt.float32
BF16 = mybir.dt.bfloat16
I32 = mybir.dt.int32
U32 = mybir.dt.uint32
U8 = mybir.dt.uint8
FP8X4 = mybir.dt.float8_e4m3fn_x4
ADD = mybir.AluOpType.add
AXIS_X = mybir.AxisListType.X

P = 128
PACK = 4
SAMPLES = 2
TOKENS = 4096
WIDTH = 512
BANKS = 8
ROWS = WIDTH // (P // BANKS)
PIECE_ROWS = (8, 8, 8, 4, 4)
EARLY_ROWS = 24
EDGE = P // BANKS
N_CHUNKS = SAMPLES * TOKENS // (PACK * P)
N_TILES = N_CHUNKS * PACK
PAIR = 2

TRANSPOSE_LEAD = 13
REGROUP_PRE_LEAD = 11
QUANTISE_PRE_LEAD = 9
FIRST_MATMUL_LEAD = 6
REGROUP_POST_LEAD = 5
QUANTISE_POST_LEAD = 4
SECOND_MATMUL_LEAD = 2

VECTOR_CHUNK = 1
HEAD_CHUNKS = 1
MEMORY_1_AFTER_CHUNK = 5
MEMORY_1_START = 13
MEMORY_1_ROWS = 4
MEMORY_1_COPY_LAG = 1
MEMORY_1_QUANTISE_LAG = 3
TP_BANKS, POST_BANKS, OUT_BANKS = 2, 3, 3

FLOPS = 2 * 2 * SAMPLES * TOKENS * WIDTH * WIDTH


def tile_proceduralmemory_pc_t_kernel(
    tc, pre, W_pm, proj_out_w_words, proj_out_w_scales, proj_out_b, out
):
    nc = tc.nc
    pre_view = pre.rearrange("b (p s) i -> b p s i", p=P)
    out_view = out.rearrange("b (p s) n -> b p s n", p=P)
    mem_view = W_pm.rearrange("b k o i -> b (k o i)").rearrange("b (p s i) -> b p s i", p=P, i=WIDTH)

    with ExitStack() as ctx:
        ctx.enter_context(tc.manual_schedule())
        const = ctx.enter_context(tc.tile_pool(name="const", bufs=1))
        mem_pool = ctx.enter_context(tc.tile_pool(name="mem", bufs=len(PIECE_ROWS)))
        pre_pool = ctx.enter_context(tc.tile_pool(name="pre", bufs=N_CHUNKS))
        quarter_pool = ctx.enter_context(tc.tile_pool(name="quarter", bufs=PACK))
        chunk_pool = ctx.enter_context(tc.tile_pool(name="chunk", bufs=4))
        pair_pool = ctx.enter_context(tc.tile_pool(name="pair", bufs=4))
        store_pool = ctx.enter_context(tc.tile_pool(name="store", bufs=28))
        tp_psum = ctx.enter_context(tc.psum_pool(name="tp", bufs=TP_BANKS))

        bias_rows = const.tile([P, WIDTH], BF16)
        nc.vector.memset(bias_rows[:], 0.0)
        ident_f32 = const.tile([P, P], F32)
        make_identity(nc, ident_f32[:])
        adder_f32 = const.tile([P, EDGE], F32)
        nc.vector.tensor_reduce(
            out=adder_f32[:], in_=ident_f32[:].rearrange("p (k e) -> p e k", e=EDGE), axis=AXIS_X, op=ADD
        )
        adder = const.tile([P, EDGE], BF16)
        nc.vector.tensor_copy(out=adder[:], in_=adder_f32[:])
        ones = const.tile([P, P], BF16)
        nc.vector.memset(ones[:], 1.0)
        w_scales = const.tile([P, WIDTH], U8, align_bytes=64)
        nc.vector.memset(w_scales[:].bitcast(I32), 0)
        w_codes = const.tile([P, WIDTH], U32, align_bytes=64)
        bias_all = const.tile([P, WIDTH], F32)
        mem_codes = [
            const.tile([P, WIDTH], U32, align_bytes=64, name="mem_codes%d" % b) for b in range(SAMPLES)
        ]
        mem_scales = [
            const.tile([P, WIDTH], U8, align_bytes=64, name="mem_scales%d" % b) for b in range(SAMPLES)
        ]

        def load_memory(b):
            rows = []
            for c, n_rows in enumerate(PIECE_ROWS):
                queue = nc.scalar if b == 0 and c % 2 == 1 else nc.sync
                piece = mem_pool.tile([P, max(PIECE_ROWS), WIDTH], BF16, name="mem_piece")
                queue.dma_start(out=piece[:, :n_rows, :], in_=mem_view[b, :, len(rows) : len(rows) + n_rows, :])
                rows.extend(piece[:, r, :] for r in range(n_rows))
            return rows

        def load_chunk(g):
            b, c = divmod(g, N_CHUNKS // SAMPLES)
            pre_sb = pre_pool.tile([P, PACK, WIDTH], BF16, name="pre_sb")
            nc.sync.dma_start(out=pre_sb[:], in_=pre_view[b, :, PACK * c : PACK * (c + 1), :])
            return pre_sb

        def load_projection():
            nc.sync.dma_start(
                out=w_codes[:].bitcast(I32),
                in_=proj_out_w_words[0].rearrange("p n t -> p (n t)").bitcast(I32),
            )
            for q in range(4):
                nc.sync.dma_start(
                    out=w_scales[32 * q : 32 * q + 4, :].bitcast(I32),
                    in_=proj_out_w_scales[0, 4 * q : 4 * q + 4, :].bitcast(I32),
                )

        w_grouped = {}

        def sum_row(rows, s, bank, at):
            for t in range(PACK):
                nc.tensor.matmul(
                    out=bank[:, t, at, :], lhsT=rows[s][:, t::PACK], rhs=adder[:], start=True, stop=True
                )

        def new_quarter(b, j):
            w_grouped[b, j] = quarter_pool.tile([P, P, PACK], BF16, align_bytes=64, name="w_grouped")

        def regroup_quarter(b, j, bank, first, count, copy):
            copy(
                out=w_grouped[b, j][:].rearrange("q (e s) t -> q e s t", s=ROWS // PACK)[:, :, first : first + count, :],
                in_=bank[:, :, :count, :].rearrange("q t s e -> q e s t"),
            )

        def quantise_quarter(b, j):
            cols = slice(j * P, (j + 1) * P)
            nc.vector.quantize_mx(
                out=mem_codes[b][:, cols].bitcast(FP8X4),
                scales=mem_scales[b][:, cols],
                in_=w_grouped[b, j][:].rearrange("q c t -> q (c t)"),
            )

        def prepare_memory_0(rows):
            for j in range(PACK):
                new_quarter(0, j)
            for lo, hi in ((0, EARLY_ROWS), (EARLY_ROWS, ROWS)):
                first, count = lo // PACK, (hi - lo) // PACK
                banks = []
                for j in range(PACK):
                    pool, name = (post_psum, "post_bank") if j < 2 else (out_psum, "out_bank")
                    banks.append(pool.tile([P, PACK, ROWS // PACK, EDGE], F32, name=name))
                for s in range(lo, hi):
                    sum_row(rows, s, banks[s % PACK], s // PACK - first)
                for j in range(PACK):
                    copy = nc.scalar.copy if j % 2 == 0 else nc.vector.tensor_copy
                    regroup_quarter(0, j, banks[j], first, count, copy)
            for j in range(PACK):
                quantise_quarter(0, j)

        mem1_banks = {}

        def memory_1_turn(n):
            per = ROWS // PACK // MEMORY_1_ROWS
            for j in range(PACK):
                first = MEMORY_1_START + j * per
                if n == first + per - 1 + MEMORY_1_QUANTISE_LAG:
                    quantise_quarter(1, j)
                if n == first + per - 1 + MEMORY_1_COPY_LAG:
                    regroup_quarter(1, j, mem1_banks[j], 0, ROWS // PACK, nc.scalar.copy)
                if first <= n < first + per:
                    if n == first:
                        new_quarter(1, j)
                        mem1_banks[j] = post_psum.tile([P, PACK, ROWS // PACK, EDGE], F32, name="post_bank")
                    for row in range((n - first) * MEMORY_1_ROWS, (n - first + 1) * MEMORY_1_ROWS):
                        sum_row(mem_rows[1], PACK * row + j, mem1_banks[j], row)

        def spread_bias():
            bias_bank = out_psum.tile([P, WIDTH], F32, name="out_bank")
            nc.tensor.matmul(out=bias_bank[:], lhsT=ones[:], rhs=bias_rows[:], start=True, stop=True)
            nc.vector.tensor_copy(out=bias_all[:], in_=bias_bank[:])

        post_psum = ctx.enter_context(tc.psum_pool(name="post", bufs=POST_BANKS))
        out_psum = ctx.enter_context(tc.psum_pool(name="outp", bufs=OUT_BANKS))

        pre_sb, mem_rows = {}, {}
        for g in range(HEAD_CHUNKS):
            pre_sb[g] = load_chunk(g)
        nc.sync.dma_start(out=bias_rows[0:1, :], in_=proj_out_b.rearrange("(o n) -> o n", o=1))
        mem_rows[0] = load_memory(0)
        for g in range(HEAD_CHUNKS, N_CHUNKS):
            pre_sb[g] = load_chunk(g)
            if g == HEAD_CHUNKS:
                load_projection()
            if g == MEMORY_1_AFTER_CHUNK:
                mem_rows[1] = load_memory(1)

        tp_banks, pre_grouped, pre_codes, pre_scales = {}, {}, {}, {}

        def transpose_chunk(g):
            if not 0 <= g < N_CHUNKS:
                return
            words = pre_sb[g][:].bitcast(F32)
            for h in range(2):
                tp_banks[g, h] = tp_psum.tile([P, 2, 2, P], F32, name="tp_bank")
                for a in range(2):
                    for u in range(2):
                        nc.tensor.transpose(
                            tp_banks[g, h][:, a, u, :],
                            words[:, 2 * h + a, u : 2 * P : 2],
                            ident_f32[:],
                        )

        def regroup_chunk(g):
            if not 0 <= g < N_CHUNKS:
                return
            pre_grouped[g] = chunk_pool.tile([P, PACK, P, PACK], BF16, align_bytes=64, name="pre_grouped")
            for h in range(2):
                copy = nc.vector.tensor_copy if g == VECTOR_CHUNK else nc.scalar.copy
                copy(
                    out=pre_grouped[g][:, 2 * h : 2 * h + 2, :, :].bitcast(F32),
                    in_=tp_banks[g, h][:].rearrange("q a u c -> q a c u"),
                )

        def quantise_chunk(g):
            if not 0 <= g < N_CHUNKS:
                return
            pre_codes[g] = chunk_pool.tile([P, PACK * P], U32, align_bytes=64, name="pre_codes")
            pre_scales[g] = chunk_pool.tile([P, PACK * P], U8, align_bytes=64, name="pre_scales")
            nc.vector.quantize_mx(
                out=pre_codes[g][:].bitcast(FP8X4),
                scales=pre_scales[g][:],
                in_=pre_grouped[g][:].rearrange("q r c t -> q (r c t)"),
            )

        post_banks, post_grouped, post_codes, post_scales = {}, {}, {}, {}
        out_banks = {}

        def first_matmul(n):
            if not 0 <= n < N_TILES:
                return
            g, r = divmod(n, PACK)
            b = g // (N_CHUNKS // SAMPLES)
            toks = slice(r * P, (r + 1) * P)
            post_banks[n] = post_psum.tile([P, PACK, P], F32, name="post_bank")
            for j in range(PACK):
                cols = slice(j * P, (j + 1) * P)
                nc.tensor.matmul_mx(
                    out=post_banks[n][:, j, :],
                    lhsT=mem_codes[b][:, cols].bitcast(FP8X4),
                    lhsT_scale=mem_scales[b][:, cols],
                    rhs=pre_codes[g][:, toks].bitcast(FP8X4),
                    rhs_scale=pre_scales[g][:, toks],
                    start=True,
                    stop=True,
                )

        def regroup_post(n):
            if not 0 <= n < N_TILES:
                return
            m, half = divmod(n, PAIR)
            if half == 0:
                post_grouped[m] = pair_pool.tile([P, PAIR, P, PACK], BF16, align_bytes=64, name="post_grouped")
            nc.scalar.copy(
                out=post_grouped[m][:, half, :, :], in_=post_banks[n][:].rearrange("p j c -> p c j")
            )

        def quantise_post(n):
            if not 0 <= n < N_TILES or n % PAIR != PAIR - 1:
                return
            m = n // PAIR
            post_codes[m] = pair_pool.tile([P, PAIR * P], U32, align_bytes=64, name="post_codes")
            post_scales[m] = pair_pool.tile([P, PAIR * P], U8, align_bytes=64, name="post_scales")
            nc.vector.quantize_mx(
                out=post_codes[m][:].bitcast(FP8X4),
                scales=post_scales[m][:],
                in_=post_grouped[m][:].rearrange("p h c j -> p (h c j)"),
            )

        def second_matmul(n):
            if not 0 <= n < N_TILES:
                return
            m, half = divmod(n, PAIR)
            toks = slice(half * P, (half + 1) * P)
            out_banks[n] = out_psum.tile([P, WIDTH], F32, name="out_bank")
            nc.tensor.matmul_mx(
                out=out_banks[n][:],
                lhsT=post_codes[m][:, toks].bitcast(FP8X4),
                lhsT_scale=post_scales[m][:, toks],
                rhs=w_codes[:].bitcast(FP8X4),
                rhs_scale=w_scales[:],
                start=True,
                stop=True,
            )

        def add_bias_and_store(n):
            if not 0 <= n < N_TILES:
                return
            b, s = divmod(n, N_TILES // SAMPLES)
            out_row = store_pool.tile([P, WIDTH], F32, name="out_row")
            nc.vector.tensor_tensor(out=out_row[:], in0=out_banks[n][:], in1=bias_all[:], op=ADD)
            nc.sync.dma_start(out=out_view[b, :, s, :], in_=out_row[:])

        for g in range(HEAD_CHUNKS):
            transpose_chunk(g)
            regroup_chunk(g)
            quantise_chunk(g)
        spread_bias()
        prepare_memory_0(mem_rows[0])

        def chunk_at(n):
            g, r = divmod(n, PACK)
            return g if r == 0 and g >= HEAD_CHUNKS else -1

        for n in range(min(PACK * HEAD_CHUNKS - TRANSPOSE_LEAD, -FIRST_MATMUL_LEAD), N_TILES):
            regroup_chunk(chunk_at(n + REGROUP_PRE_LEAD))
            quantise_chunk(chunk_at(n + QUANTISE_PRE_LEAD))
            second_matmul(n + SECOND_MATMUL_LEAD)
            first_matmul(n + FIRST_MATMUL_LEAD)
            transpose_chunk(chunk_at(n + TRANSPOSE_LEAD))
            memory_1_turn(n)
            regroup_post(n + REGROUP_POST_LEAD)
            add_bias_and_store(n)
            quantise_post(n + QUANTISE_POST_LEAD)
